import numpy as np
import ml_dtypes


def mxq(x, axis, fmt="e4m3"):
    dtype, down = {"e4m3": (ml_dtypes.float8_e4m3fn, 7), "e5m2": (ml_dtypes.float8_e5m2, 14)}[fmt]
    v = np.moveaxis(np.asarray(x, np.float32).astype(ml_dtypes.bfloat16).astype(np.float64), axis, -1)
    blocks = v.reshape(v.shape[:-1] + (-1, 32))
    amax = np.abs(blocks).max(-1, keepdims=True)
    byte = np.maximum(np.where(amax > 0, np.frexp(amax)[1] - 1 + 127, 0) - down, 1)
    scale = np.exp2(byte - 127.0)
    codes = (blocks / scale).astype(np.float32).astype(dtype).astype(np.float64)
    return np.moveaxis((codes * scale).reshape(v.shape), -1, axis)


WIDE = False


def mx_kscale(k):
    if not WIDE:
        return np.ones(k)
    levels = np.array([10, -10, 5, -5, 0])
    a = np.random.permutation(np.resize(levels, k // 512 * 4)).reshape(k // 512, 4)
    idx = np.arange(k)
    return np.exp2(a[idx // 512, idx % 128 // 32])


BF16 = ml_dtypes.bfloat16


def bf(x):
    return np.asarray(x, np.float32).astype(BF16)


def f64(x):
    return np.asarray(x).astype(np.float64)


B, C, T, DK, DV, P = 1, 1024, 2048, 128, 512, 4


def maxpool(y):
    b, ch, t = y.shape
    return y.reshape(b, ch, t // P, P).max(axis=-1)


def setup_inputs():
    s = mx_kscale(C)
    return {"x": bf(np.random.standard_normal((B, C, T)) * s[:, None]),
            "Wq": bf(np.random.standard_normal((DK, C)) * 0.5 / np.sqrt(C) / s),
            "Wk": bf(np.random.standard_normal((DK, C)) * 0.5 / np.sqrt(C) / s),
            "Wv": bf(np.random.standard_normal((DV, C)) / np.sqrt(C) / s)}


def reference(x, Wq, Wk, Wv):
    xq = mxq(f64(x), 1, "e4m3")
    q = mxq(f64(Wq), 1, "e4m3") @ xq
    k = maxpool(mxq(f64(Wk), 1, "e4m3") @ xq)
    v = maxpool(mxq(f64(Wv), 1, "e4m3") @ xq)
    return q, k, v

@@ -1,0 +1,132 @@
+from contextlib import ExitStack
+
+import concourse.mybir as mybir
+from concourse.masks import make_identity
+
+F32 = mybir.dt.float32
+BF16 = mybir.dt.bfloat16
+U32 = mybir.dt.uint32
+U8 = mybir.dt.uint8
+FP8X4 = mybir.dt.float8_e4m3fn_x4
+
+P = 128
+PACK = 4
+K_PASS = P * PACK
+PAIR = 2
+T_BLOCK = 512
+WINDOW = 4
+RUN = 4
+
+FLOPS = 2 * (128 + 128 + 512) * 1024 * 2048
+
+
+def tile_selfattention_pa_kernel(tc, x, Wq, Wk, Wv, out_0, out_1, out_2):
+    nc = tc.nc
+    channels, steps = x.shape[1], x.shape[2]
+    passes = channels // K_PASS
+    t_blocks = steps // T_BLOCK
+    v_blocks = Wv.shape[0] // P
+    row_blocks = 2 + v_blocks
+    pooled_cols = T_BLOCK // WINDOW
+
+    with ExitStack() as ctx:
+        keep = ctx.enter_context(tc.tile_pool(name="keep", bufs=1))
+        banks = ctx.enter_context(tc.psum_pool(name="banks", bufs=8))
+
+        identity = keep.tile([P, P], F32)
+        make_identity(nc, identity[:])
+
+        def load_x(n, c):
+            raw = keep.tile([P, PACK, T_BLOCK], BF16, name="x_raw_%d_%d" % (n, c))
+            nc.sync.dma_start(
+                out=raw[:],
+                in_=x[
+                    0, c * K_PASS : (c + 1) * K_PASS, n * T_BLOCK : (n + 1) * T_BLOCK
+                ].rearrange("(p j) t -> p j t", j=PACK),
+            )
+            return raw
+
+        w_raw = keep.tile([P, row_blocks, channels], BF16)
+        x_raw = {}
+        x_raw[0, 0] = load_x(0, 0)
+        nc.sync.dma_start(out=w_raw[:, 0, :], in_=Wq)
+        nc.sync.dma_start(out=w_raw[:, 1, :], in_=Wk)
+        x_raw[0, 1] = load_x(0, 1)
+        nc.sync.dma_start(out=w_raw[:, 2:, :], in_=Wv.rearrange("(b p) k -> p b k", p=P))
+        for n in range(1, t_blocks):
+            for c in range(passes):
+                x_raw[n, c] = load_x(n, c)
+
+        w_codes = keep.tile([P, row_blocks, passes, P], U32, align_bytes=64)
+        w_scales = keep.tile([P, row_blocks, passes, P], U8, align_bytes=64)
+        for b in range(row_blocks):
+            words = (
+                w_raw[:, b, :]
+                .bitcast(F32)
+                .rearrange("r (c p u) -> r c u p", c=passes, u=PAIR)
+            )
+            flipped = banks.tile([P, passes, PAIR, P], F32, tag="bank", name="flipped_%d" % b)
+            for c in range(passes):
+                for u in range(PAIR):
+                    nc.tensor.transpose(flipped[:, c, u, :], words[:, c, u, :], identity[:])
+            w_grouped = keep.tile(
+                [P, passes, P, PACK], BF16, align_bytes=64, name="w_grouped_%d" % b
+            )
+            nc.vector.tensor_copy(
+                out=w_grouped[:].bitcast(F32), in_=flipped[:].rearrange("p c u r -> p c r u")
+            )
+            nc.vector.quantize_mx(
+                out=w_codes[:, b].rearrange("p c r -> p (c r)").bitcast(FP8X4),
+                scales=w_scales[:, b].rearrange("p c r -> p (c r)"),
+                in_=w_grouped[:].rearrange("p c r j -> p (c r j)"),
+            )
+
+        x_codes = keep.tile([P, t_blocks, passes, T_BLOCK], U32, align_bytes=64)
+        x_scales = keep.tile([P, t_blocks, passes, T_BLOCK], U8, align_bytes=64)
+        v_rows = out_2[0].rearrange("(b p) w -> p b w", p=P)
+        for n in range(t_blocks):
+            for c in range(passes):
+                x_grouped = keep.tile(
+                    [P, T_BLOCK, PACK], BF16, align_bytes=64, name="x_grouped_%d_%d" % (n, c)
+                )
+                nc.scalar.copy(
+                    out=x_grouped[:].rearrange("p (g i) j -> p g j i", i=RUN),
+                    in_=x_raw[n, c][:].rearrange("p j (g i) -> p g j i", i=RUN),
+                )
+                nc.vector.quantize_mx(
+                    out=x_codes[:, n, c, :].bitcast(FP8X4),
+                    scales=x_scales[:, n, c, :],
+                    in_=x_grouped[:].rearrange("p t j -> p (t j)"),
+                )
+
+            sums = [
+                banks.tile([P, T_BLOCK], F32, tag="bank", name="sums_%d_%d" % (n, b))
+                for b in range(row_blocks)
+            ]
+            for c in range(passes):
+                for b in range(row_blocks):
+                    nc.tensor.matmul_mx(
+                        out=sums[b][:],
+                        lhsT=w_codes[:, b, c, :].bitcast(FP8X4),
+                        lhsT_scale=w_scales[:, b, c, :],
+                        rhs=x_codes[:, n, c, :].bitcast(FP8X4),
+                        rhs_scale=x_scales[:, n, c, :],
+                        start=(c == 0),
+                        stop=(c == passes - 1),
+                    )
+
+            q_part = keep.tile([P, T_BLOCK], F32, name="q_part_%d" % n)
+            nc.scalar.copy(out=q_part[:], in_=sums[0][:])
+            nc.sync.dma_start(out=out_0[0, :, n * T_BLOCK : (n + 1) * T_BLOCK], in_=q_part[:])
+
+            pooled = keep.tile([P, row_blocks - 1, pooled_cols], F32, name="pooled_%d" % n)
+            for b in range(1, row_blocks):
+                nc.vector.tensor_reduce(
+                    out=pooled[:, b - 1, :],
+                    in_=sums[b][:].rearrange("p (w i) -> p w i", i=WINDOW),
+                    axis=mybir.AxisListType.X,
+                    op=mybir.AluOpType.max,
+                )
+            w_cols = slice(n * pooled_cols, (n + 1) * pooled_cols)
+            nc.sync.dma_start(out=out_1[0, :, w_cols], in_=pooled[:, 0, :])
+            nc.sync.dma_start(out=v_rows[:, :, w_cols], in_=pooled[:, 1:, :])

@@ -16,6 +16,8 @@ PAIR = 2
 T_BLOCK = 512
 WINDOW = 4
 RUN = 4
+VECTOR_ROUNDS = 2
+BANKS = 8
 
 FLOPS = 2 * (128 + 128 + 512) * 1024 * 2048
 
@@ -24,55 +26,84 @@ def tile_selfattention_pa_kernel(tc, x, Wq, Wk, Wv, out_0, out_1, out_2):
     nc = tc.nc
     channels, steps = x.shape[1], x.shape[2]
     passes = channels // K_PASS
-    t_blocks = steps // T_BLOCK
-    v_blocks = Wv.shape[0] // P
-    row_blocks = 2 + v_blocks
+    rounds = steps // T_BLOCK
     pooled_cols = T_BLOCK // WINDOW
+    w_blocks = [Wq, Wk] + [Wv[r : r + P, :] for r in range(0, Wv.shape[0], P)]
+    row_blocks = len(w_blocks)
+    spare_banks = BANKS - row_blocks
 
     with ExitStack() as ctx:
         keep = ctx.enter_context(tc.tile_pool(name="keep", bufs=1))
-        banks = ctx.enter_context(tc.psum_pool(name="banks", bufs=8))
+        psum = ctx.enter_context(tc.psum_pool(name="psum", bufs=1))
+        ctx.enter_context(tc.manual_schedule())
+
+        def bank(shape, index):
+            return psum.tile(shape, F32, tag="bank_%d" % (index % BANKS), name="bank_use_%d" % index)
 
         identity = keep.tile([P, P], F32)
         make_identity(nc, identity[:])
 
-        def load_x(n, c):
-            raw = keep.tile([P, PACK, T_BLOCK], BF16, name="x_raw_%d_%d" % (n, c))
-            nc.sync.dma_start(
-                out=raw[:],
-                in_=x[
-                    0, c * K_PASS : (c + 1) * K_PASS, n * T_BLOCK : (n + 1) * T_BLOCK
-                ].rearrange("(p j) t -> p j t", j=PACK),
-            )
-            return raw
+        x_raw = {}
+
+        def load_x(n):
+            for c in range(passes):
+                x_raw[n, c] = keep.tile([P, PACK, T_BLOCK], BF16, name="x_raw_%d_%d" % (n, c))
+                nc.sync.dma_start(
+                    out=x_raw[n, c][:],
+                    in_=x[
+                        0, c * K_PASS : (c + 1) * K_PASS, n * T_BLOCK : (n + 1) * T_BLOCK
+                    ].rearrange("(p j) t -> p j t", j=PACK),
+                )
 
         w_raw = keep.tile([P, row_blocks, channels], BF16)
-        x_raw = {}
-        x_raw[0, 0] = load_x(0, 0)
-        nc.sync.dma_start(out=w_raw[:, 0, :], in_=Wq)
-        nc.sync.dma_start(out=w_raw[:, 1, :], in_=Wk)
-        x_raw[0, 1] = load_x(0, 1)
-        nc.sync.dma_start(out=w_raw[:, 2:, :], in_=Wv.rearrange("(b p) k -> p b k", p=P))
-        for n in range(1, t_blocks):
+        load_x(0)
+        for b in range(row_blocks):
+            nc.sync.dma_start(out=w_raw[:, b, :], in_=w_blocks[b])
+        for n in range(1, rounds):
+            load_x(n)
+
+        x_grouped = {}
+        x_codes = keep.tile([P, rounds, passes, T_BLOCK], U32, align_bytes=64)
+        x_scales = keep.tile([P, rounds, passes, T_BLOCK], U8, align_bytes=64)
+
+        def regroup_x(n):
             for c in range(passes):
-                x_raw[n, c] = load_x(n, c)
+                x_grouped[n, c] = keep.tile(
+                    [P, T_BLOCK, PACK], BF16, align_bytes=64, name="x_grouped_%d_%d" % (n, c)
+                )
+                copy = nc.scalar.copy
+                if n < VECTOR_ROUNDS and c == passes - 1:
+                    copy = nc.vector.tensor_copy
+                copy(
+                    out=x_grouped[n, c][:].rearrange("p (g i) j -> p g j i", i=RUN),
+                    in_=x_raw[n, c][:].rearrange("p j (g i) -> p g j i", i=RUN),
+                )
+
+        def quantise_x(n):
+            for c in range(passes):
+                nc.vector.quantize_mx(
+                    out=x_codes[:, n, c, :].bitcast(FP8X4),
+                    scales=x_scales[:, n, c, :],
+                    in_=x_grouped[n, c][:].rearrange("p t j -> p (t j)"),
+                )
 
         w_codes = keep.tile([P, row_blocks, passes, P], U32, align_bytes=64)
         w_scales = keep.tile([P, row_blocks, passes, P], U8, align_bytes=64)
-        for b in range(row_blocks):
+
+        def quantise_w(b):
             words = (
                 w_raw[:, b, :]
                 .bitcast(F32)
                 .rearrange("r (c p u) -> r c u p", c=passes, u=PAIR)
             )
-            flipped = banks.tile([P, passes, PAIR, P], F32, tag="bank", name="flipped_%d" % b)
+            flipped = bank([P, passes, PAIR, P], b)
             for c in range(passes):
                 for u in range(PAIR):
                     nc.tensor.transpose(flipped[:, c, u, :], words[:, c, u, :], identity[:])
             w_grouped = keep.tile(
                 [P, passes, P, PACK], BF16, align_bytes=64, name="w_grouped_%d" % b
             )
-            nc.vector.tensor_copy(
+            nc.scalar.copy(
                 out=w_grouped[:].bitcast(F32), in_=flipped[:].rearrange("p c u r -> p c r u")
             )
             nc.vector.quantize_mx(
@@ -81,32 +112,16 @@ def tile_selfattention_pa_kernel(tc, x, Wq, Wk, Wv, out_0, out_1, out_2):
                 in_=w_grouped[:].rearrange("p c r j -> p (c r j)"),
             )
 
-        x_codes = keep.tile([P, t_blocks, passes, T_BLOCK], U32, align_bytes=64)
-        x_scales = keep.tile([P, t_blocks, passes, T_BLOCK], U8, align_bytes=64)
+        sums = {}
+        pooled = {}
         v_rows = out_2[0].rearrange("(b p) w -> p b w", p=P)
-        for n in range(t_blocks):
-            for c in range(passes):
-                x_grouped = keep.tile(
-                    [P, T_BLOCK, PACK], BF16, align_bytes=64, name="x_grouped_%d_%d" % (n, c)
-                )
-                nc.scalar.copy(
-                    out=x_grouped[:].rearrange("p (g i) j -> p g j i", i=RUN),
-                    in_=x_raw[n, c][:].rearrange("p j (g i) -> p g j i", i=RUN),
-                )
-                nc.vector.quantize_mx(
-                    out=x_codes[:, n, c, :].bitcast(FP8X4),
-                    scales=x_scales[:, n, c, :],
-                    in_=x_grouped[:].rearrange("p t j -> p (t j)"),
-                )
 
-            sums = [
-                banks.tile([P, T_BLOCK], F32, tag="bank", name="sums_%d_%d" % (n, b))
-                for b in range(row_blocks)
-            ]
-            for c in range(passes):
-                for b in range(row_blocks):
+        def multiply(n):
+            for b in range(row_blocks):
+                sums[n, b] = bank([P, T_BLOCK], (n + 1) * row_blocks + b)
+                for c in range(passes):
                     nc.tensor.matmul_mx(
-                        out=sums[b][:],
+                        out=sums[n, b][:],
                         lhsT=w_codes[:, b, c, :].bitcast(FP8X4),
                         lhsT_scale=w_scales[:, b, c, :],
                         rhs=x_codes[:, n, c, :].bitcast(FP8X4),
@@ -115,18 +130,38 @@ def tile_selfattention_pa_kernel(tc, x, Wq, Wk, Wv, out_0, out_1, out_2):
                         stop=(c == passes - 1),
                     )
 
+        def store_q(n):
             q_part = keep.tile([P, T_BLOCK], F32, name="q_part_%d" % n)
-            nc.scalar.copy(out=q_part[:], in_=sums[0][:])
+            nc.scalar.copy(out=q_part[:], in_=sums[n, 0][:])
             nc.sync.dma_start(out=out_0[0, :, n * T_BLOCK : (n + 1) * T_BLOCK], in_=q_part[:])
 
-            pooled = keep.tile([P, row_blocks - 1, pooled_cols], F32, name="pooled_%d" % n)
-            for b in range(1, row_blocks):
+        def pool(n, blocks):
+            for b in blocks:
                 nc.vector.tensor_reduce(
-                    out=pooled[:, b - 1, :],
-                    in_=sums[b][:].rearrange("p (w i) -> p w i", i=WINDOW),
+                    out=pooled[n][:, b - 1, :],
+                    in_=sums[n, b][:].rearrange("p (w i) -> p w i", i=WINDOW),
                     axis=mybir.AxisListType.X,
                     op=mybir.AluOpType.max,
                 )
+
+        def store_pooled(n):
             w_cols = slice(n * pooled_cols, (n + 1) * pooled_cols)
-            nc.sync.dma_start(out=out_1[0, :, w_cols], in_=pooled[:, 0, :])
-            nc.sync.dma_start(out=v_rows[:, :, w_cols], in_=pooled[:, 1:, :])
+            nc.sync.dma_start(out=out_1[0, :, w_cols], in_=pooled[n][:, 0, :])
+            nc.sync.dma_start(out=v_rows[:, :, w_cols], in_=pooled[n][:, 1:, :])
+
+        regroup_x(0)
+        quantise_x(0)
+        for b in range(row_blocks):
+            quantise_w(b)
+        multiply(0)
+        for n in range(rounds):
+            pooled[n] = keep.tile([P, row_blocks - 1, pooled_cols], F32, name="pooled_%d" % n)
+            if n + 1 < rounds:
+                regroup_x(n + 1)
+            store_q(n)
+            pool(n, range(1, row_blocks - spare_banks))
+            if n + 1 < rounds:
+                quantise_x(n + 1)
+                multiply(n + 1)
+            pool(n, range(row_blocks - spare_banks, row_blocks))
+            store_pooled(n)

@@ -114,7 +114,7 @@ def tile_selfattention_pa_kernel(tc, x, Wq, Wk, Wv, out_0, out_1, out_2):
 
         sums = {}
         pooled = {}
-        v_rows = out_2[0].rearrange("(b p) w -> p b w", p=P)
+        pooled_out = [out_1[0]] + [out_2[0, r : r + P, :] for r in range(0, Wv.shape[0], P)]
 
         def multiply(n):
             for b in range(row_blocks):
@@ -143,11 +143,10 @@ def tile_selfattention_pa_kernel(tc, x, Wq, Wk, Wv, out_0, out_1, out_2):
                     axis=mybir.AxisListType.X,
                     op=mybir.AluOpType.max,
                 )
-
-        def store_pooled(n):
-            w_cols = slice(n * pooled_cols, (n + 1) * pooled_cols)
-            nc.sync.dma_start(out=out_1[0, :, w_cols], in_=pooled[n][:, 0, :])
-            nc.sync.dma_start(out=v_rows[:, :, w_cols], in_=pooled[n][:, 1:, :])
+                nc.sync.dma_start(
+                    out=pooled_out[b - 1][:, n * pooled_cols : (n + 1) * pooled_cols],
+                    in_=pooled[n][:, b - 1, :],
+                )
 
         regroup_x(0)
         quantise_x(0)
@@ -164,4 +163,3 @@ def tile_selfattention_pa_kernel(tc, x, Wq, Wk, Wv, out_0, out_1, out_2):
                 quantise_x(n + 1)
                 multiply(n + 1)
             pool(n, range(row_blocks - spare_banks, row_blocks))
-            store_pooled(n)

@@ -16,8 +16,9 @@ PAIR = 2
 T_BLOCK = 512
 WINDOW = 4
 RUN = 4
-VECTOR_ROUNDS = 2
 BANKS = 8
+VECTOR_STEPS = 320
+GPSIMD_STEPS = 256
 
 FLOPS = 2 * (128 + 128 + 512) * 1024 * 2048
 
@@ -31,6 +32,8 @@ def tile_selfattention_pa_kernel(tc, x, Wq, Wk, Wv, out_0, out_1, out_2):
     w_blocks = [Wq, Wk] + [Wv[r : r + P, :] for r in range(0, Wv.shape[0], P)]
     row_blocks = len(w_blocks)
     spare_banks = BANKS - row_blocks
+    first_order = list(range(1, row_blocks)) + [0]
+    later_order = list(range(row_blocks))
 
     with ExitStack() as ctx:
         keep = ctx.enter_context(tc.tile_pool(name="keep", bufs=1))
@@ -57,7 +60,7 @@ def tile_selfattention_pa_kernel(tc, x, Wq, Wk, Wv, out_0, out_1, out_2):
 
         w_raw = keep.tile([P, row_blocks, channels], BF16)
         load_x(0)
-        for b in range(row_blocks):
+        for b in first_order:
             nc.sync.dma_start(out=w_raw[:, b, :], in_=w_blocks[b])
         for n in range(1, rounds):
             load_x(n)
@@ -66,18 +69,37 @@ def tile_selfattention_pa_kernel(tc, x, Wq, Wk, Wv, out_0, out_1, out_2):
         x_codes = keep.tile([P, rounds, passes, T_BLOCK], U32, align_bytes=64)
         x_scales = keep.tile([P, rounds, passes, T_BLOCK], U8, align_bytes=64)
 
+        def regroup_steps(copy, n, c, lo, hi):
+            copy(
+                out=x_grouped[n, c][:, lo:hi, :].rearrange("p (g i) j -> p g j i", i=RUN),
+                in_=x_raw[n, c][:, :, lo:hi].rearrange("p j (g i) -> p g j i", i=RUN),
+            )
+
         def regroup_x(n):
             for c in range(passes):
+                if n > 0 and c == passes - 1:
+                    x_grouped[n, c] = keep.tile(
+                        [P, T_BLOCK, PACK], BF16, align_bytes=64,
+                        tag="x_grouped_shared", name="x_grouped_%d_%d" % (n, c),
+                    )
+                    nc.gpsimd.tensor_scalar(
+                        out=x_grouped[n, c][:, 0:GPSIMD_STEPS, :],
+                        in0=x_raw[n, c][:, :, 0:GPSIMD_STEPS].rearrange("p j t -> p t j"),
+                        scalar1=1.0,
+                        scalar2=0.0,
+                        op0=mybir.AluOpType.mult,
+                        op1=mybir.AluOpType.add,
+                    )
+                    regroup_steps(nc.scalar.copy, n, c, GPSIMD_STEPS, T_BLOCK)
+                    continue
                 x_grouped[n, c] = keep.tile(
                     [P, T_BLOCK, PACK], BF16, align_bytes=64, name="x_grouped_%d_%d" % (n, c)
                 )
-                copy = nc.scalar.copy
-                if n < VECTOR_ROUNDS and c == passes - 1:
-                    copy = nc.vector.tensor_copy
-                copy(
-                    out=x_grouped[n, c][:].rearrange("p (g i) j -> p g j i", i=RUN),
-                    in_=x_raw[n, c][:].rearrange("p j (g i) -> p g j i", i=RUN),
-                )
+                if n == 0:
+                    regroup_steps(nc.vector.tensor_copy, n, c, 0, VECTOR_STEPS)
+                    regroup_steps(nc.scalar.copy, n, c, VECTOR_STEPS, T_BLOCK)
+                else:
+                    regroup_steps(nc.scalar.copy, n, c, 0, T_BLOCK)
 
         def quantise_x(n):
             for c in range(passes):
@@ -90,13 +112,13 @@ def tile_selfattention_pa_kernel(tc, x, Wq, Wk, Wv, out_0, out_1, out_2):
         w_codes = keep.tile([P, row_blocks, passes, P], U32, align_bytes=64)
         w_scales = keep.tile([P, row_blocks, passes, P], U8, align_bytes=64)
 
-        def quantise_w(b):
+        def quantise_w(place, b):
             words = (
                 w_raw[:, b, :]
                 .bitcast(F32)
                 .rearrange("r (c p u) -> r c u p", c=passes, u=PAIR)
             )
-            flipped = bank([P, passes, PAIR, P], b)
+            flipped = bank([P, passes, PAIR, P], place)
             for c in range(passes):
                 for u in range(PAIR):
                     nc.tensor.transpose(flipped[:, c, u, :], words[:, c, u, :], identity[:])
@@ -116,9 +138,9 @@ def tile_selfattention_pa_kernel(tc, x, Wq, Wk, Wv, out_0, out_1, out_2):
         pooled = {}
         pooled_out = [out_1[0]] + [out_2[0, r : r + P, :] for r in range(0, Wv.shape[0], P)]
 
-        def multiply(n):
-            for b in range(row_blocks):
-                sums[n, b] = bank([P, T_BLOCK], (n + 1) * row_blocks + b)
+        def multiply(n, order):
+            for place, b in enumerate(order):
+                sums[n, b] = bank([P, T_BLOCK], (n + 1) * row_blocks + place)
                 for c in range(passes):
                     nc.tensor.matmul_mx(
                         out=sums[n, b][:],
@@ -130,13 +152,15 @@ def tile_selfattention_pa_kernel(tc, x, Wq, Wk, Wv, out_0, out_1, out_2):
                         stop=(c == passes - 1),
                     )
 
-        def store_q(n):
-            q_part = keep.tile([P, T_BLOCK], F32, name="q_part_%d" % n)
-            nc.scalar.copy(out=q_part[:], in_=sums[n, 0][:])
-            nc.sync.dma_start(out=out_0[0, :, n * T_BLOCK : (n + 1) * T_BLOCK], in_=q_part[:])
-
-        def pool(n, blocks):
+        def empty(n, blocks):
             for b in blocks:
+                if b == 0:
+                    q_part = keep.tile([P, T_BLOCK], F32, name="q_part_%d" % n)
+                    nc.scalar.copy(out=q_part[:], in_=sums[n, 0][:])
+                    nc.sync.dma_start(
+                        out=out_0[0, :, n * T_BLOCK : (n + 1) * T_BLOCK], in_=q_part[:]
+                    )
+                    continue
                 nc.vector.tensor_reduce(
                     out=pooled[n][:, b - 1, :],
                     in_=sums[n, b][:].rearrange("p (w i) -> p w i", i=WINDOW),
@@ -150,16 +174,17 @@ def tile_selfattention_pa_kernel(tc, x, Wq, Wk, Wv, out_0, out_1, out_2):
 
         regroup_x(0)
         quantise_x(0)
-        for b in range(row_blocks):
-            quantise_w(b)
-        multiply(0)
+        for place, b in enumerate(first_order):
+            quantise_w(place, b)
+        multiply(0, first_order)
+        regroup_x(1)
         for n in range(rounds):
+            order = first_order if n == 0 else later_order
             pooled[n] = keep.tile([P, row_blocks - 1, pooled_cols], F32, name="pooled_%d" % n)
-            if n + 1 < rounds:
-                regroup_x(n + 1)
-            store_q(n)
-            pool(n, range(1, row_blocks - spare_banks))
+            empty(n, order[: row_blocks - spare_banks])
             if n + 1 < rounds:
                 quantise_x(n + 1)
-                multiply(n + 1)
-            pool(n, range(row_blocks - spare_banks, row_blocks))
+                multiply(n + 1, later_order)
+            if n + 2 < rounds:
+                regroup_x(n + 2)
+            empty(n, order[row_blocks - spare_banks :])

@@ -19,6 +19,7 @@ RUN = 4
 BANKS = 8
 VECTOR_STEPS = 320
 GPSIMD_STEPS = 256
+EARLY_BLOCKS = 3
 
 FLOPS = 2 * (128 + 128 + 512) * 1024 * 2048
 
@@ -59,8 +60,10 @@ def tile_selfattention_pa_kernel(tc, x, Wq, Wk, Wv, out_0, out_1, out_2):
                 )
 
         w_raw = keep.tile([P, row_blocks, channels], BF16)
+        for b in first_order[:EARLY_BLOCKS]:
+            nc.sync.dma_start(out=w_raw[:, b, :], in_=w_blocks[b])
         load_x(0)
-        for b in first_order:
+        for b in first_order[EARLY_BLOCKS:]:
             nc.sync.dma_start(out=w_raw[:, b, :], in_=w_blocks[b])
         for n in range(1, rounds):
             load_x(n)
@@ -172,10 +175,12 @@ def tile_selfattention_pa_kernel(tc, x, Wq, Wk, Wv, out_0, out_1, out_2):
                     in_=pooled[n][:, b - 1, :],
                 )
 
+        for place in range(EARLY_BLOCKS):
+            quantise_w(place, first_order[place])
         regroup_x(0)
         quantise_x(0)
-        for place, b in enumerate(first_order):
-            quantise_w(place, b)
+        for place in range(EARLY_BLOCKS, row_blocks):
+            quantise_w(place, first_order[place])
         multiply(0, first_order)
         regroup_x(1)
         for n in range(rounds):

@@ -18,7 +18,7 @@ WINDOW = 4
 RUN = 4
 BANKS = 8
 VECTOR_STEPS = 320
-GPSIMD_STEPS = 256
+GPSIMD_STEPS = 384
 EARLY_BLOCKS = 3
 
 FLOPS = 2 * (128 + 128 + 512) * 1024 * 2048

@@ -20,6 +20,7 @@ BANKS = 8
 VECTOR_STEPS = 320
 GPSIMD_STEPS = 384
 EARLY_BLOCKS = 3
+READ_FIRST = 3
 
 FLOPS = 2 * (128 + 128 + 512) * 1024 * 2048
 
@@ -33,7 +34,7 @@ def tile_selfattention_pa_kernel(tc, x, Wq, Wk, Wv, out_0, out_1, out_2):
     w_blocks = [Wq, Wk] + [Wv[r : r + P, :] for r in range(0, Wv.shape[0], P)]
     row_blocks = len(w_blocks)
     spare_banks = BANKS - row_blocks
-    first_order = list(range(1, row_blocks)) + [0]
+    first_order = list(range(1, row_blocks - spare_banks)) + [0] + list(range(row_blocks - spare_banks, row_blocks))
     later_order = list(range(row_blocks))
 
     with ExitStack() as ctx:
@@ -141,8 +142,9 @@ def tile_selfattention_pa_kernel(tc, x, Wq, Wk, Wv, out_0, out_1, out_2):
         pooled = {}
         pooled_out = [out_1[0]] + [out_2[0, r : r + P, :] for r in range(0, Wv.shape[0], P)]
 
-        def multiply(n, order):
-            for place, b in enumerate(order):
+        def multiply(n, order, places):
+            for place in places:
+                b = order[place]
                 sums[n, b] = bank([P, T_BLOCK], (n + 1) * row_blocks + place)
                 for c in range(passes):
                     nc.tensor.matmul_mx(
@@ -181,15 +183,18 @@ def tile_selfattention_pa_kernel(tc, x, Wq, Wk, Wv, out_0, out_1, out_2):
         quantise_x(0)
         for place in range(EARLY_BLOCKS, row_blocks):
             quantise_w(place, first_order[place])
-        multiply(0, first_order)
+        multiply(0, first_order, range(row_blocks))
         regroup_x(1)
         for n in range(rounds):
             order = first_order if n == 0 else later_order
             pooled[n] = keep.tile([P, row_blocks - 1, pooled_cols], F32, name="pooled_%d" % n)
-            empty(n, order[: row_blocks - spare_banks])
+            empty(n, order[:READ_FIRST])
             if n + 1 < rounds:
                 quantise_x(n + 1)
-                multiply(n + 1, later_order)
+                multiply(n + 1, later_order, range(READ_FIRST + spare_banks))
             if n + 2 < rounds:
                 regroup_x(n + 2)
-            empty(n, order[row_blocks - spare_banks :])
+            for place in range(READ_FIRST, row_blocks):
+                empty(n, [order[place]])
+                if n + 1 < rounds and place + spare_banks < row_blocks:
+                    multiply(n + 1, later_order, [place + spare_banks])

@@ -19,7 +19,8 @@ RUN = 4
 BANKS = 8
 VECTOR_STEPS = 320
 GPSIMD_STEPS = 384
-EARLY_BLOCKS = 3
+EARLY_BLOCKS = 2
+W_JOIN = 2
 READ_FIRST = 3
 
 FLOPS = 2 * (128 + 128 + 512) * 1024 * 2048
@@ -35,7 +36,7 @@ def tile_selfattention_pa_kernel(tc, x, Wq, Wk, Wv, out_0, out_1, out_2):
     row_blocks = len(w_blocks)
     spare_banks = BANKS - row_blocks
     first_order = list(range(1, row_blocks - spare_banks)) + [0] + list(range(row_blocks - spare_banks, row_blocks))
-    later_order = list(range(row_blocks))
+    later_order = [1, 2, 0, 3, 4, 5]
 
     with ExitStack() as ctx:
         keep = ctx.enter_context(tc.tile_pool(name="keep", bufs=1))
@@ -50,24 +51,25 @@ def tile_selfattention_pa_kernel(tc, x, Wq, Wk, Wv, out_0, out_1, out_2):
 
         x_raw = {}
 
-        def load_x(n):
-            for c in range(passes):
-                x_raw[n, c] = keep.tile([P, PACK, T_BLOCK], BF16, name="x_raw_%d_%d" % (n, c))
-                nc.sync.dma_start(
-                    out=x_raw[n, c][:],
-                    in_=x[
-                        0, c * K_PASS : (c + 1) * K_PASS, n * T_BLOCK : (n + 1) * T_BLOCK
-                    ].rearrange("(p j) t -> p j t", j=PACK),
-                )
+        def load_x(n, c):
+            x_raw[n, c] = keep.tile([P, PACK, T_BLOCK], BF16, name="x_raw_%d_%d" % (n, c))
+            nc.sync.dma_start(
+                out=x_raw[n, c][:],
+                in_=x[
+                    0, c * K_PASS : (c + 1) * K_PASS, n * T_BLOCK : (n + 1) * T_BLOCK
+                ].rearrange("(p j) t -> p j t", j=PACK),
+            )
 
         w_raw = keep.tile([P, row_blocks, channels], BF16)
+        load_x(0, 0)
         for b in first_order[:EARLY_BLOCKS]:
             nc.sync.dma_start(out=w_raw[:, b, :], in_=w_blocks[b])
-        load_x(0)
+        load_x(0, 1)
         for b in first_order[EARLY_BLOCKS:]:
             nc.sync.dma_start(out=w_raw[:, b, :], in_=w_blocks[b])
         for n in range(1, rounds):
-            load_x(n)
+            for c in range(passes):
+                load_x(n, c)
 
         x_grouped = {}
         x_codes = keep.tile([P, rounds, passes, T_BLOCK], U32, align_bytes=64)
@@ -79,8 +81,8 @@ def tile_selfattention_pa_kernel(tc, x, Wq, Wk, Wv, out_0, out_1, out_2):
                 in_=x_raw[n, c][:, :, lo:hi].rearrange("p j (g i) -> p g j i", i=RUN),
             )
 
-        def regroup_x(n):
-            for c in range(passes):
+        def regroup_x(n, pieces):
+            for c in pieces:
                 if n > 0 and c == passes - 1:
                     x_grouped[n, c] = keep.tile(
                         [P, T_BLOCK, PACK], BF16, align_bytes=64,
@@ -105,8 +107,8 @@ def tile_selfattention_pa_kernel(tc, x, Wq, Wk, Wv, out_0, out_1, out_2):
                 else:
                     regroup_steps(nc.scalar.copy, n, c, 0, T_BLOCK)
 
-        def quantise_x(n):
-            for c in range(passes):
+        def quantise_x(n, pieces):
+            for c in pieces:
                 nc.vector.quantize_mx(
                     out=x_codes[:, n, c, :].bitcast(FP8X4),
                     scales=x_scales[:, n, c, :],
@@ -115,27 +117,33 @@ def tile_selfattention_pa_kernel(tc, x, Wq, Wk, Wv, out_0, out_1, out_2):
 
         w_codes = keep.tile([P, row_blocks, passes, P], U32, align_bytes=64)
         w_scales = keep.tile([P, row_blocks, passes, P], U8, align_bytes=64)
+        w_grouped = {}
 
-        def quantise_w(place, b):
-            words = (
-                w_raw[:, b, :]
-                .bitcast(F32)
-                .rearrange("r (c p u) -> r c u p", c=passes, u=PAIR)
+        def quantise_w(first_place):
+            places = range(first_place, first_place + W_JOIN)
+            w_grouped[first_place] = keep.tile(
+                [P, W_JOIN, passes, P, PACK], BF16, align_bytes=64, name="w_grouped_%d" % first_place
             )
-            flipped = bank([P, passes, PAIR, P], place)
-            for c in range(passes):
-                for u in range(PAIR):
-                    nc.tensor.transpose(flipped[:, c, u, :], words[:, c, u, :], identity[:])
-            w_grouped = keep.tile(
-                [P, passes, P, PACK], BF16, align_bytes=64, name="w_grouped_%d" % b
-            )
-            nc.scalar.copy(
-                out=w_grouped[:].bitcast(F32), in_=flipped[:].rearrange("p c u r -> p c r u")
-            )
+            for place in places:
+                words = (
+                    w_raw[:, first_order[place], :]
+                    .bitcast(F32)
+                    .rearrange("r (c p u) -> r c u p", c=passes, u=PAIR)
+                )
+                flipped = bank([P, passes, PAIR, P], place)
+                for c in range(passes):
+                    for u in range(PAIR):
+                        nc.tensor.transpose(flipped[:, c, u, :], words[:, c, u, :], identity[:])
+                nc.scalar.copy(
+                    out=w_grouped[first_place][:, place - first_place].bitcast(F32),
+                    in_=flipped[:].rearrange("p c u r -> p c r u"),
+                )
             nc.vector.quantize_mx(
-                out=w_codes[:, b].rearrange("p c r -> p (c r)").bitcast(FP8X4),
-                scales=w_scales[:, b].rearrange("p c r -> p (c r)"),
-                in_=w_grouped[:].rearrange("p c r j -> p (c r j)"),
+                out=w_codes[:, first_place : first_place + W_JOIN]
+                .rearrange("p b c r -> p (b c r)")
+                .bitcast(FP8X4),
+                scales=w_scales[:, first_place : first_place + W_JOIN].rearrange("p b c r -> p (b c r)"),
+                in_=w_grouped[first_place][:].rearrange("p b c r j -> p (b c r j)"),
             )
 
         sums = {}
@@ -149,8 +157,8 @@ def tile_selfattention_pa_kernel(tc, x, Wq, Wk, Wv, out_0, out_1, out_2):
                 for c in range(passes):
                     nc.tensor.matmul_mx(
                         out=sums[n, b][:],
-                        lhsT=w_codes[:, b, c, :].bitcast(FP8X4),
-                        lhsT_scale=w_scales[:, b, c, :],
+                        lhsT=w_codes[:, first_order.index(b), c, :].bitcast(FP8X4),
+                        lhsT_scale=w_scales[:, first_order.index(b), c, :],
                         rhs=x_codes[:, n, c, :].bitcast(FP8X4),
                         rhs_scale=x_scales[:, n, c, :],
                         start=(c == 0),
@@ -177,23 +185,25 @@ def tile_selfattention_pa_kernel(tc, x, Wq, Wk, Wv, out_0, out_1, out_2):
                     in_=pooled[n][:, b - 1, :],
                 )
 
-        for place in range(EARLY_BLOCKS):
-            quantise_w(place, first_order[place])
-        regroup_x(0)
-        quantise_x(0)
-        for place in range(EARLY_BLOCKS, row_blocks):
-            quantise_w(place, first_order[place])
+        regroup_x(0, [0])
+        quantise_x(0, [0])
+        for place in range(0, EARLY_BLOCKS, W_JOIN):
+            quantise_w(place)
+        regroup_x(0, [1])
+        quantise_x(0, [1])
+        for place in range(EARLY_BLOCKS, row_blocks, W_JOIN):
+            quantise_w(place)
         multiply(0, first_order, range(row_blocks))
-        regroup_x(1)
+        regroup_x(1, range(passes))
         for n in range(rounds):
             order = first_order if n == 0 else later_order
             pooled[n] = keep.tile([P, row_blocks - 1, pooled_cols], F32, name="pooled_%d" % n)
             empty(n, order[:READ_FIRST])
             if n + 1 < rounds:
-                quantise_x(n + 1)
+                quantise_x(n + 1, range(passes))
                 multiply(n + 1, later_order, range(READ_FIRST + spare_banks))
             if n + 2 < rounds:
-                regroup_x(n + 2)
+                regroup_x(n + 2, range(passes))
             for place in range(READ_FIRST, row_blocks):
                 empty(n, [order[place]])
                 if n + 1 < rounds and place + spare_banks < row_blocks:

@@ -13,6 +13,7 @@ P = 128
 PACK = 4
 K_PASS = P * PACK
 PAIR = 2
+HALVES = PACK // PAIR
 T_BLOCK = 512
 WINDOW = 4
 RUN = 4
@@ -48,17 +49,22 @@ def tile_selfattention_pa_kernel(tc, x, Wq, Wk, Wv, out_0, out_1, out_2):
 
         identity = keep.tile([P, P], F32)
         make_identity(nc, identity[:])
+        first_copy = keep.tile([P, 2], F32)
+        nc.vector.memset(first_copy[:], 0.0)
+        nc.scalar.copy(out=first_copy[:, 1:2], in_=first_copy[:, 0:1])
 
         x_raw = {}
 
         def load_x(n, c):
             x_raw[n, c] = keep.tile([P, PACK, T_BLOCK], BF16, name="x_raw_%d_%d" % (n, c))
-            nc.sync.dma_start(
-                out=x_raw[n, c][:],
-                in_=x[
-                    0, c * K_PASS : (c + 1) * K_PASS, n * T_BLOCK : (n + 1) * T_BLOCK
-                ].rearrange("(p j) t -> p j t", j=PACK),
-            )
+            for u in range(HALVES):
+                first = c * K_PASS + u * P * PAIR
+                nc.sync.dma_start(
+                    out=x_raw[n, c][:, u * PAIR : (u + 1) * PAIR, :],
+                    in_=x[0, first : first + P * PAIR, n * T_BLOCK : (n + 1) * T_BLOCK].rearrange(
+                        "(p e) t -> p e t", e=PAIR
+                    ),
+                )
 
         w_raw = keep.tile([P, row_blocks, channels], BF16)
         load_x(0, 0)
@@ -128,11 +134,11 @@ def tile_selfattention_pa_kernel(tc, x, Wq, Wk, Wv, out_0, out_1, out_2):
                 words = (
                     w_raw[:, first_order[place], :]
                     .bitcast(F32)
-                    .rearrange("r (c p u) -> r c u p", c=passes, u=PAIR)
+                    .rearrange("r (c u p) -> r c u p", c=passes, u=HALVES)
                 )
-                flipped = bank([P, passes, PAIR, P], place)
+                flipped = bank([P, passes, HALVES, P], place)
                 for c in range(passes):
-                    for u in range(PAIR):
+                    for u in range(HALVES):
                         nc.tensor.transpose(flipped[:, c, u, :], words[:, c, u, :], identity[:])
                 nc.scalar.copy(
                     out=w_grouped[first_place][:, place - first_place].bitcast(F32),

@@ -19,10 +19,8 @@ WINDOW = 4
 RUN = 4
 BANKS = 8
 VECTOR_STEPS = 320
-GPSIMD_STEPS = 384
-EARLY_BLOCKS = 2
-W_JOIN = 2
-READ_FIRST = 3
+GPSIMD_STEPS = {1: 256, 2: 384, 3: 384}
+W_GROUPS = [(1, 2), (3, 4), (5,), (0,)]
 
 FLOPS = 2 * (128 + 128 + 512) * 1024 * 2048
 
@@ -35,9 +33,7 @@ def tile_selfattention_pa_kernel(tc, x, Wq, Wk, Wv, out_0, out_1, out_2):
     pooled_cols = T_BLOCK // WINDOW
     w_blocks = [Wq, Wk] + [Wv[r : r + P, :] for r in range(0, Wv.shape[0], P)]
     row_blocks = len(w_blocks)
-    spare_banks = BANKS - row_blocks
-    first_order = list(range(1, row_blocks - spare_banks)) + [0] + list(range(row_blocks - spare_banks, row_blocks))
-    later_order = [1, 2, 0, 3, 4, 5]
+    w_order = [b for group in W_GROUPS for b in group]
 
     with ExitStack() as ctx:
         keep = ctx.enter_context(tc.tile_pool(name="keep", bufs=1))
@@ -67,13 +63,20 @@ def tile_selfattention_pa_kernel(tc, x, Wq, Wk, Wv, out_0, out_1, out_2):
                 )
 
         w_raw = keep.tile([P, row_blocks, channels], BF16)
+
+        def load_w(blocks):
+            for b in blocks:
+                nc.sync.dma_start(out=w_raw[:, b, :], in_=w_blocks[b])
+
         load_x(0, 0)
-        for b in first_order[:EARLY_BLOCKS]:
-            nc.sync.dma_start(out=w_raw[:, b, :], in_=w_blocks[b])
+        load_w(W_GROUPS[0])
         load_x(0, 1)
-        for b in first_order[EARLY_BLOCKS:]:
-            nc.sync.dma_start(out=w_raw[:, b, :], in_=w_blocks[b])
-        for n in range(1, rounds):
+        load_w(W_GROUPS[1])
+        load_w(W_GROUPS[2])
+        load_x(1, 0)
+        load_x(1, 1)
+        load_w(W_GROUPS[3])
+        for n in range(2, rounds):
             for c in range(passes):
                 load_x(n, c)
 
@@ -95,14 +98,14 @@ def tile_selfattention_pa_kernel(tc, x, Wq, Wk, Wv, out_0, out_1, out_2):
                         tag="x_grouped_shared", name="x_grouped_%d_%d" % (n, c),
                     )
                     nc.gpsimd.tensor_scalar(
-                        out=x_grouped[n, c][:, 0:GPSIMD_STEPS, :],
-                        in0=x_raw[n, c][:, :, 0:GPSIMD_STEPS].rearrange("p j t -> p t j"),
+                        out=x_grouped[n, c][:, 0 : GPSIMD_STEPS[n], :],
+                        in0=x_raw[n, c][:, :, 0 : GPSIMD_STEPS[n]].rearrange("p j t -> p t j"),
                         scalar1=1.0,
                         scalar2=0.0,
                         op0=mybir.AluOpType.mult,
                         op1=mybir.AluOpType.add,
                     )
-                    regroup_steps(nc.scalar.copy, n, c, GPSIMD_STEPS, T_BLOCK)
+                    regroup_steps(nc.scalar.copy, n, c, GPSIMD_STEPS[n], T_BLOCK)
                     continue
                 x_grouped[n, c] = keep.tile(
                     [P, T_BLOCK, PACK], BF16, align_bytes=64, name="x_grouped_%d_%d" % (n, c)
@@ -125,46 +128,52 @@ def tile_selfattention_pa_kernel(tc, x, Wq, Wk, Wv, out_0, out_1, out_2):
         w_scales = keep.tile([P, row_blocks, passes, P], U8, align_bytes=64)
         w_grouped = {}
 
-        def quantise_w(first_place):
-            places = range(first_place, first_place + W_JOIN)
-            w_grouped[first_place] = keep.tile(
-                [P, W_JOIN, passes, P, PACK], BF16, align_bytes=64, name="w_grouped_%d" % first_place
+        bank_uses = []
+
+        def next_bank(shape):
+            bank_uses.append(shape)
+            return bank(shape, len(bank_uses) - 1)
+
+        def transpose_w(group):
+            w_grouped[group] = keep.tile(
+                [P, len(group), passes, P, PACK], BF16, align_bytes=64, name="w_grouped_%d" % group[0]
             )
-            for place in places:
+            for place, b in enumerate(group):
                 words = (
-                    w_raw[:, first_order[place], :]
+                    w_raw[:, b, :]
                     .bitcast(F32)
                     .rearrange("r (c u p) -> r c u p", c=passes, u=HALVES)
                 )
-                flipped = bank([P, passes, HALVES, P], place)
+                flipped = next_bank([P, passes, HALVES, P])
                 for c in range(passes):
                     for u in range(HALVES):
                         nc.tensor.transpose(flipped[:, c, u, :], words[:, c, u, :], identity[:])
                 nc.scalar.copy(
-                    out=w_grouped[first_place][:, place - first_place].bitcast(F32),
+                    out=w_grouped[group][:, place].bitcast(F32),
                     in_=flipped[:].rearrange("p c u r -> p c r u"),
                 )
+
+        def quantise_w(group):
+            lo = w_order.index(group[0])
+            hi = lo + len(group)
             nc.vector.quantize_mx(
-                out=w_codes[:, first_place : first_place + W_JOIN]
-                .rearrange("p b c r -> p (b c r)")
-                .bitcast(FP8X4),
-                scales=w_scales[:, first_place : first_place + W_JOIN].rearrange("p b c r -> p (b c r)"),
-                in_=w_grouped[first_place][:].rearrange("p b c r j -> p (b c r j)"),
+                out=w_codes[:, lo:hi].rearrange("p b c r -> p (b c r)").bitcast(FP8X4),
+                scales=w_scales[:, lo:hi].rearrange("p b c r -> p (b c r)"),
+                in_=w_grouped[group][:].rearrange("p b c r j -> p (b c r j)"),
             )
 
         sums = {}
         pooled = {}
         pooled_out = [out_1[0]] + [out_2[0, r : r + P, :] for r in range(0, Wv.shape[0], P)]
 
-        def multiply(n, order, places):
-            for place in places:
-                b = order[place]
-                sums[n, b] = bank([P, T_BLOCK], (n + 1) * row_blocks + place)
+        def multiply(n, blocks):
+            for b in blocks:
+                sums[n, b] = next_bank([P, T_BLOCK])
                 for c in range(passes):
                     nc.tensor.matmul_mx(
                         out=sums[n, b][:],
-                        lhsT=w_codes[:, first_order.index(b), c, :].bitcast(FP8X4),
-                        lhsT_scale=w_scales[:, first_order.index(b), c, :],
+                        lhsT=w_codes[:, w_order.index(b), c, :].bitcast(FP8X4),
+                        lhsT_scale=w_scales[:, w_order.index(b), c, :],
                         rhs=x_codes[:, n, c, :].bitcast(FP8X4),
                         rhs_scale=x_scales[:, n, c, :],
                         start=(c == 0),
@@ -191,26 +200,46 @@ def tile_selfattention_pa_kernel(tc, x, Wq, Wk, Wv, out_0, out_1, out_2):
                     in_=pooled[n][:, b - 1, :],
                 )
 
+        for n in range(rounds):
+            pooled[n] = keep.tile([P, row_blocks - 1, pooled_cols], F32, name="pooled_%d" % n)
         regroup_x(0, [0])
         quantise_x(0, [0])
-        for place in range(0, EARLY_BLOCKS, W_JOIN):
-            quantise_w(place)
+        transpose_w(W_GROUPS[0])
         regroup_x(0, [1])
+        quantise_w(W_GROUPS[0])
         quantise_x(0, [1])
-        for place in range(EARLY_BLOCKS, row_blocks, W_JOIN):
-            quantise_w(place)
-        multiply(0, first_order, range(row_blocks))
+        transpose_w(W_GROUPS[1])
+        quantise_w(W_GROUPS[1])
+        transpose_w(W_GROUPS[2])
+        quantise_w(W_GROUPS[2])
+        multiply(0, [1, 2, 3, 4])
         regroup_x(1, range(passes))
-        for n in range(rounds):
-            order = first_order if n == 0 else later_order
-            pooled[n] = keep.tile([P, row_blocks - 1, pooled_cols], F32, name="pooled_%d" % n)
-            empty(n, order[:READ_FIRST])
-            if n + 1 < rounds:
-                quantise_x(n + 1, range(passes))
-                multiply(n + 1, later_order, range(READ_FIRST + spare_banks))
-            if n + 2 < rounds:
-                regroup_x(n + 2, range(passes))
-            for place in range(READ_FIRST, row_blocks):
-                empty(n, [order[place]])
-                if n + 1 < rounds and place + spare_banks < row_blocks:
-                    multiply(n + 1, later_order, [place + spare_banks])
+        transpose_w(W_GROUPS[3])
+        multiply(0, [5])
+        empty(0, [1, 2, 3])
+        quantise_x(1, range(passes))
+        quantise_w(W_GROUPS[3])
+        multiply(1, [1, 2, 3])
+        multiply(0, [0])
+        multiply(1, [0])
+        regroup_x(2, range(passes))
+        empty(0, [4])
+        multiply(1, [4, 5])
+        empty(0, [5])
+        empty(1, [1, 2])
+        quantise_x(2, range(passes))
+        multiply(2, [1, 2, 0])
+        empty(0, [0])
+        empty(1, [0, 3])
+        multiply(2, [3, 4, 5])
+        regroup_x(3, range(passes))
+        empty(1, [4, 5])
+        empty(2, [1, 2])
+        quantise_x(3, range(passes))
+        multiply(3, [1, 2, 0, 3])
+        empty(2, [0])
+        multiply(3, [4])
+        empty(2, [3])
+        multiply(3, [5])
+        empty(2, [4, 5])
+        empty(3, [1, 2, 0, 3, 4, 5])

@@ -18,9 +18,11 @@ T_BLOCK = 512
 WINDOW = 4
 RUN = 4
 BANKS = 8
-VECTOR_STEPS = 320
-GPSIMD_STEPS = {1: 256, 2: 384, 3: 384}
+VECTOR_STEPS = {(0, 0): 320, (0, 1): 320, (1, 0): 128}
+GPSIMD_STEPS = {1: 256, 2: 256, 3: 384}
 W_GROUPS = [(1, 2), (3, 4), (5,), (0,)]
+
+WARM_UP = [6, 4]
 
 FLOPS = 2 * (128 + 128 + 512) * 1024 * 2048
 
@@ -48,6 +50,9 @@ def tile_selfattention_pa_kernel(tc, x, Wq, Wk, Wv, out_0, out_1, out_2):
         first_copy = keep.tile([P, 2], F32)
         nc.vector.memset(first_copy[:], 0.0)
         nc.scalar.copy(out=first_copy[:, 1:2], in_=first_copy[:, 0:1])
+
+        zeros = keep.tile([P, T_BLOCK], BF16)
+        nc.vector.memset(zeros[:], 0.0)
 
         x_raw = {}
 
@@ -110,11 +115,10 @@ def tile_selfattention_pa_kernel(tc, x, Wq, Wk, Wv, out_0, out_1, out_2):
                 x_grouped[n, c] = keep.tile(
                     [P, T_BLOCK, PACK], BF16, align_bytes=64, name="x_grouped_%d_%d" % (n, c)
                 )
-                if n == 0:
-                    regroup_steps(nc.vector.tensor_copy, n, c, 0, VECTOR_STEPS)
-                    regroup_steps(nc.scalar.copy, n, c, VECTOR_STEPS, T_BLOCK)
-                else:
-                    regroup_steps(nc.scalar.copy, n, c, 0, T_BLOCK)
+                vector_steps = VECTOR_STEPS.get((n, c), 0)
+                if vector_steps:
+                    regroup_steps(nc.vector.tensor_copy, n, c, 0, vector_steps)
+                regroup_steps(nc.scalar.copy, n, c, vector_steps, T_BLOCK)
 
         def quantise_x(n, pieces):
             for c in pieces:
@@ -133,6 +137,12 @@ def tile_selfattention_pa_kernel(tc, x, Wq, Wk, Wv, out_0, out_1, out_2):
         def next_bank(shape):
             bank_uses.append(shape)
             return bank(shape, len(bank_uses) - 1)
+
+        unread = next_bank([P, T_BLOCK])
+
+        def warm_up(products):
+            for i in range(products):
+                nc.tensor.matmul(unread[:], zeros[:, 0:P], zeros[:], start=True, stop=True)
 
         def transpose_w(group):
             w_grouped[group] = keep.tile(
@@ -204,7 +214,9 @@ def tile_selfattention_pa_kernel(tc, x, Wq, Wk, Wv, out_0, out_1, out_2):
             pooled[n] = keep.tile([P, row_blocks - 1, pooled_cols], F32, name="pooled_%d" % n)
         regroup_x(0, [0])
         quantise_x(0, [0])
+        warm_up(WARM_UP[0])
         transpose_w(W_GROUPS[0])
+        warm_up(WARM_UP[1])
         regroup_x(0, [1])
         quantise_w(W_GROUPS[0])
         quantise_x(0, [1])

@@ -19,10 +19,10 @@ WINDOW = 4
 RUN = 4
 BANKS = 8
 VECTOR_STEPS = {(0, 0): 320, (0, 1): 320, (1, 0): 128}
-GPSIMD_STEPS = {1: 256, 2: 256, 3: 384}
-W_GROUPS = [(1, 2), (3, 4), (5,), (0,)]
+GPSIMD_STEPS = 256
+W_GROUPS = [(1, 2), (3, 4), (5, 0)]
 
-WARM_UP = [6, 4]
+WARM_UP = [7, 4, 1]
 
 FLOPS = 2 * (128 + 128 + 512) * 1024 * 2048
 
@@ -77,10 +77,9 @@ def tile_selfattention_pa_kernel(tc, x, Wq, Wk, Wv, out_0, out_1, out_2):
         load_w(W_GROUPS[0])
         load_x(0, 1)
         load_w(W_GROUPS[1])
-        load_w(W_GROUPS[2])
         load_x(1, 0)
         load_x(1, 1)
-        load_w(W_GROUPS[3])
+        load_w(W_GROUPS[2])
         for n in range(2, rounds):
             for c in range(passes):
                 load_x(n, c)
@@ -103,14 +102,14 @@ def tile_selfattention_pa_kernel(tc, x, Wq, Wk, Wv, out_0, out_1, out_2):
                         tag="x_grouped_shared", name="x_grouped_%d_%d" % (n, c),
                     )
                     nc.gpsimd.tensor_scalar(
-                        out=x_grouped[n, c][:, 0 : GPSIMD_STEPS[n], :],
-                        in0=x_raw[n, c][:, :, 0 : GPSIMD_STEPS[n]].rearrange("p j t -> p t j"),
+                        out=x_grouped[n, c][:, 0 : GPSIMD_STEPS, :],
+                        in0=x_raw[n, c][:, :, 0 : GPSIMD_STEPS].rearrange("p j t -> p t j"),
                         scalar1=1.0,
                         scalar2=0.0,
                         op0=mybir.AluOpType.mult,
                         op1=mybir.AluOpType.add,
                     )
-                    regroup_steps(nc.scalar.copy, n, c, GPSIMD_STEPS[n], T_BLOCK)
+                    regroup_steps(nc.scalar.copy, n, c, GPSIMD_STEPS, T_BLOCK)
                     continue
                 x_grouped[n, c] = keep.tile(
                     [P, T_BLOCK, PACK], BF16, align_bytes=64, name="x_grouped_%d_%d" % (n, c)
@@ -176,19 +175,23 @@ def tile_selfattention_pa_kernel(tc, x, Wq, Wk, Wv, out_0, out_1, out_2):
         pooled = {}
         pooled_out = [out_1[0]] + [out_2[0, r : r + P, :] for r in range(0, Wv.shape[0], P)]
 
-        def multiply(n, blocks):
+        def multiply(n, blocks, pass_by_pass=False):
             for b in blocks:
                 sums[n, b] = next_bank([P, T_BLOCK])
-                for c in range(passes):
-                    nc.tensor.matmul_mx(
-                        out=sums[n, b][:],
-                        lhsT=w_codes[:, w_order.index(b), c, :].bitcast(FP8X4),
-                        lhsT_scale=w_scales[:, w_order.index(b), c, :],
-                        rhs=x_codes[:, n, c, :].bitcast(FP8X4),
-                        rhs_scale=x_scales[:, n, c, :],
-                        start=(c == 0),
-                        stop=(c == passes - 1),
-                    )
+            if pass_by_pass:
+                order = [(b, c) for c in range(passes) for b in blocks]
+            else:
+                order = [(b, c) for b in blocks for c in range(passes)]
+            for b, c in order:
+                nc.tensor.matmul_mx(
+                    out=sums[n, b][:],
+                    lhsT=w_codes[:, w_order.index(b), c, :].bitcast(FP8X4),
+                    lhsT_scale=w_scales[:, w_order.index(b), c, :],
+                    rhs=x_codes[:, n, c, :].bitcast(FP8X4),
+                    rhs_scale=x_scales[:, n, c, :],
+                    start=(c == 0),
+                    stop=(c == passes - 1),
+                )
 
         def empty(n, blocks):
             for b in blocks:
@@ -221,31 +224,34 @@ def tile_selfattention_pa_kernel(tc, x, Wq, Wk, Wv, out_0, out_1, out_2):
         quantise_w(W_GROUPS[0])
         quantise_x(0, [1])
         transpose_w(W_GROUPS[1])
+        warm_up(WARM_UP[2])
+        regroup_x(1, [0])
         quantise_w(W_GROUPS[1])
+        multiply(0, [1, 2, 3])
+        regroup_x(1, [1])
         transpose_w(W_GROUPS[2])
-        quantise_w(W_GROUPS[2])
-        multiply(0, [1, 2, 3, 4])
-        regroup_x(1, range(passes))
-        transpose_w(W_GROUPS[3])
-        multiply(0, [5])
+        multiply(0, [4])
         empty(0, [1, 2, 3])
         quantise_x(1, range(passes))
-        quantise_w(W_GROUPS[3])
-        multiply(1, [1, 2, 3])
-        multiply(0, [0])
-        multiply(1, [0])
-        regroup_x(2, range(passes))
         empty(0, [4])
-        multiply(1, [4, 5])
+        quantise_w(W_GROUPS[2])
+        multiply(1, [1, 2], pass_by_pass=True)
+        multiply(1, [3])
+        multiply(0, [5])
+        multiply(1, [4])
+        multiply(0, [0])
+        multiply(1, [5, 0])
+        regroup_x(2, range(passes))
+        empty(1, [1, 2, 3])
         empty(0, [5])
-        empty(1, [1, 2])
         quantise_x(2, range(passes))
-        multiply(2, [1, 2, 0])
-        empty(0, [0])
-        empty(1, [0, 3])
-        multiply(2, [3, 4, 5])
         regroup_x(3, range(passes))
-        empty(1, [4, 5])
+        multiply(2, [1, 2], pass_by_pass=True)
+        empty(0, [0])
+        empty(1, [4])
+        multiply(2, [0, 3, 4])
+        empty(1, [0, 5])
+        multiply(2, [5])
         empty(2, [1, 2])
         quantise_x(3, range(passes))
         multiply(3, [1, 2, 0, 3])

@@ -22,7 +22,7 @@ VECTOR_STEPS = {(0, 0): 320, (0, 1): 320, (1, 0): 128}
 GPSIMD_STEPS = 256
 W_GROUPS = [(1, 2), (3, 4), (5, 0)]
 
-WARM_UP = [7, 4, 1]
+WARM_UP = [7, 4]
 
 FLOPS = 2 * (128 + 128 + 512) * 1024 * 2048
 
@@ -85,8 +85,8 @@ def tile_selfattention_pa_kernel(tc, x, Wq, Wk, Wv, out_0, out_1, out_2):
                 load_x(n, c)
 
         x_grouped = {}
-        x_codes = keep.tile([P, rounds, passes, T_BLOCK], U32, align_bytes=64)
-        x_scales = keep.tile([P, rounds, passes, T_BLOCK], U8, align_bytes=64)
+        x_codes = keep.tile([P, rounds, passes, T_BLOCK], U32, align_bytes=256)
+        x_scales = keep.tile([P, rounds, passes, T_BLOCK], U8, align_bytes=256)
 
         def regroup_steps(copy, n, c, lo, hi):
             copy(
@@ -98,7 +98,7 @@ def tile_selfattention_pa_kernel(tc, x, Wq, Wk, Wv, out_0, out_1, out_2):
             for c in pieces:
                 if n > 0 and c == passes - 1:
                     x_grouped[n, c] = keep.tile(
-                        [P, T_BLOCK, PACK], BF16, align_bytes=64,
+                        [P, T_BLOCK, PACK], BF16, align_bytes=256,
                         tag="x_grouped_shared", name="x_grouped_%d_%d" % (n, c),
                     )
                     nc.gpsimd.tensor_scalar(
@@ -112,7 +112,7 @@ def tile_selfattention_pa_kernel(tc, x, Wq, Wk, Wv, out_0, out_1, out_2):
                     regroup_steps(nc.scalar.copy, n, c, GPSIMD_STEPS, T_BLOCK)
                     continue
                 x_grouped[n, c] = keep.tile(
-                    [P, T_BLOCK, PACK], BF16, align_bytes=64, name="x_grouped_%d_%d" % (n, c)
+                    [P, T_BLOCK, PACK], BF16, align_bytes=256, name="x_grouped_%d_%d" % (n, c)
                 )
                 vector_steps = VECTOR_STEPS.get((n, c), 0)
                 if vector_steps:
@@ -127,8 +127,8 @@ def tile_selfattention_pa_kernel(tc, x, Wq, Wk, Wv, out_0, out_1, out_2):
                     in_=x_grouped[n, c][:].rearrange("p t j -> p (t j)"),
                 )
 
-        w_codes = keep.tile([P, row_blocks, passes, P], U32, align_bytes=64)
-        w_scales = keep.tile([P, row_blocks, passes, P], U8, align_bytes=64)
+        w_codes = keep.tile([P, row_blocks, passes, P], U32, align_bytes=256)
+        w_scales = keep.tile([P, row_blocks, passes, P], U8, align_bytes=256)
         w_grouped = {}
 
         bank_uses = []
@@ -145,7 +145,7 @@ def tile_selfattention_pa_kernel(tc, x, Wq, Wk, Wv, out_0, out_1, out_2):
 
         def transpose_w(group):
             w_grouped[group] = keep.tile(
-                [P, len(group), passes, P, PACK], BF16, align_bytes=64, name="w_grouped_%d" % group[0]
+                [P, len(group), passes, P, PACK], BF16, align_bytes=256, name="w_grouped_%d" % group[0]
             )
             for place, b in enumerate(group):
                 words = (
@@ -175,14 +175,10 @@ def tile_selfattention_pa_kernel(tc, x, Wq, Wk, Wv, out_0, out_1, out_2):
         pooled = {}
         pooled_out = [out_1[0]] + [out_2[0, r : r + P, :] for r in range(0, Wv.shape[0], P)]
 
-        def multiply(n, blocks, pass_by_pass=False):
+        def multiply_pass(n, blocks, c):
             for b in blocks:
-                sums[n, b] = next_bank([P, T_BLOCK])
-            if pass_by_pass:
-                order = [(b, c) for c in range(passes) for b in blocks]
-            else:
-                order = [(b, c) for b in blocks for c in range(passes)]
-            for b, c in order:
+                if c == 0:
+                    sums[n, b] = next_bank([P, T_BLOCK])
                 nc.tensor.matmul_mx(
                     out=sums[n, b][:],
                     lhsT=w_codes[:, w_order.index(b), c, :].bitcast(FP8X4),
@@ -192,6 +188,15 @@ def tile_selfattention_pa_kernel(tc, x, Wq, Wk, Wv, out_0, out_1, out_2):
                     start=(c == 0),
                     stop=(c == passes - 1),
                 )
+
+        def multiply(n, blocks):
+            for b in blocks:
+                for c in range(passes):
+                    multiply_pass(n, [b], c)
+
+        def multiply_pass_by_pass(n, blocks):
+            for c in range(passes):
+                multiply_pass(n, blocks, c)
 
         def empty(n, blocks):
             for b in blocks:
@@ -224,18 +229,19 @@ def tile_selfattention_pa_kernel(tc, x, Wq, Wk, Wv, out_0, out_1, out_2):
         quantise_w(W_GROUPS[0])
         quantise_x(0, [1])
         transpose_w(W_GROUPS[1])
-        warm_up(WARM_UP[2])
         regroup_x(1, [0])
         quantise_w(W_GROUPS[1])
-        multiply(0, [1, 2, 3])
+        multiply_pass_by_pass(0, [1, 2])
+        multiply(0, [3])
         regroup_x(1, [1])
+        multiply_pass(0, [4], 0)
         transpose_w(W_GROUPS[2])
-        multiply(0, [4])
+        multiply_pass(0, [4], 1)
         empty(0, [1, 2, 3])
         quantise_x(1, range(passes))
         empty(0, [4])
         quantise_w(W_GROUPS[2])
-        multiply(1, [1, 2], pass_by_pass=True)
+        multiply_pass_by_pass(1, [1, 2])
         multiply(1, [3])
         multiply(0, [5])
         multiply(1, [4])
@@ -246,7 +252,7 @@ def tile_selfattention_pa_kernel(tc, x, Wq, Wk, Wv, out_0, out_1, out_2):
         empty(0, [5])
         quantise_x(2, range(passes))
         regroup_x(3, range(passes))
-        multiply(2, [1, 2], pass_by_pass=True)
+        multiply_pass_by_pass(2, [1, 2])
         empty(0, [0])
         empty(1, [4])
         multiply(2, [0, 3, 4])

from contextlib import ExitStack

import concourse.mybir as mybir
from concourse.masks import make_identity

F32 = mybir.dt.float32
BF16 = mybir.dt.bfloat16
U32 = mybir.dt.uint32
U8 = mybir.dt.uint8
FP8X4 = mybir.dt.float8_e4m3fn_x4

P = 128
PACK = 4
K_PASS = P * PACK
PAIR = 2
HALVES = PACK // PAIR
T_BLOCK = 512
WINDOW = 4
RUN = 4
BANKS = 8
VECTOR_STEPS = {(0, 0): 320, (0, 1): 320, (1, 0): 128}
GPSIMD_STEPS = 256
W_GROUPS = [(1, 2), (3, 4), (5, 0)]

WARM_UP = [7, 4]

FLOPS = 2 * (128 + 128 + 512) * 1024 * 2048


def tile_selfattention_pa_kernel(tc, x, Wq, Wk, Wv, out_0, out_1, out_2):
    nc = tc.nc
    channels, steps = x.shape[1], x.shape[2]
    passes = channels // K_PASS
    rounds = steps // T_BLOCK
    pooled_cols = T_BLOCK // WINDOW
    w_blocks = [Wq, Wk] + [Wv[r : r + P, :] for r in range(0, Wv.shape[0], P)]
    row_blocks = len(w_blocks)
    w_order = [b for group in W_GROUPS for b in group]

    with ExitStack() as ctx:
        keep = ctx.enter_context(tc.tile_pool(name="keep", bufs=1))
        psum = ctx.enter_context(tc.psum_pool(name="psum", bufs=1))
        ctx.enter_context(tc.manual_schedule())

        def bank(shape, index):
            return psum.tile(shape, F32, tag="bank_%d" % (index % BANKS), name="bank_use_%d" % index)

        identity = keep.tile([P, P], F32)
        make_identity(nc, identity[:])
        first_copy = keep.tile([P, 2], F32)
        nc.vector.memset(first_copy[:], 0.0)
        nc.scalar.copy(out=first_copy[:, 1:2], in_=first_copy[:, 0:1])

        zeros = keep.tile([P, T_BLOCK], BF16)
        nc.vector.memset(zeros[:], 0.0)

        x_raw = {}

        def load_x(n, c):
            x_raw[n, c] = keep.tile([P, PACK, T_BLOCK], BF16, name="x_raw_%d_%d" % (n, c))
            for u in range(HALVES):
                first = c * K_PASS + u * P * PAIR
                nc.sync.dma_start(
                    out=x_raw[n, c][:, u * PAIR : (u + 1) * PAIR, :],
                    in_=x[0, first : first + P * PAIR, n * T_BLOCK : (n + 1) * T_BLOCK].rearrange(
                        "(p e) t -> p e t", e=PAIR
                    ),
                )

        w_raw = keep.tile([P, row_blocks, channels], BF16)

        def load_w(blocks):
            for b in blocks:
                nc.sync.dma_start(out=w_raw[:, b, :], in_=w_blocks[b])

        load_x(0, 0)
        load_w(W_GROUPS[0])
        load_x(0, 1)
        load_w(W_GROUPS[1])
        load_x(1, 0)
        load_x(1, 1)
        load_w(W_GROUPS[2])
        for n in range(2, rounds):
            for c in range(passes):
                load_x(n, c)

        x_grouped = {}
        x_codes = keep.tile([P, rounds, passes, T_BLOCK], U32, align_bytes=256)
        x_scales = keep.tile([P, rounds, passes, T_BLOCK], U8, align_bytes=256)

        def regroup_steps(copy, n, c, lo, hi):
            copy(
                out=x_grouped[n, c][:, lo:hi, :].rearrange("p (g i) j -> p g j i", i=RUN),
                in_=x_raw[n, c][:, :, lo:hi].rearrange("p j (g i) -> p g j i", i=RUN),
            )

        def regroup_x(n, pieces):
            for c in pieces:
                if n > 0 and c == passes - 1:
                    x_grouped[n, c] = keep.tile(
                        [P, T_BLOCK, PACK], BF16, align_bytes=256,
                        tag="x_grouped_shared", name="x_grouped_%d_%d" % (n, c),
                    )
                    nc.gpsimd.tensor_scalar(
                        out=x_grouped[n, c][:, 0 : GPSIMD_STEPS, :],
                        in0=x_raw[n, c][:, :, 0 : GPSIMD_STEPS].rearrange("p j t -> p t j"),
                        scalar1=1.0,
                        scalar2=0.0,
                        op0=mybir.AluOpType.mult,
                        op1=mybir.AluOpType.add,
                    )
                    regroup_steps(nc.scalar.copy, n, c, GPSIMD_STEPS, T_BLOCK)
                    continue
                x_grouped[n, c] = keep.tile(
                    [P, T_BLOCK, PACK], BF16, align_bytes=256, name="x_grouped_%d_%d" % (n, c)
                )
                vector_steps = VECTOR_STEPS.get((n, c), 0)
                if vector_steps:
                    regroup_steps(nc.vector.tensor_copy, n, c, 0, vector_steps)
                regroup_steps(nc.scalar.copy, n, c, vector_steps, T_BLOCK)

        def quantise_x(n, pieces):
            for c in pieces:
                nc.vector.quantize_mx(
                    out=x_codes[:, n, c, :].bitcast(FP8X4),
                    scales=x_scales[:, n, c, :],
                    in_=x_grouped[n, c][:].rearrange("p t j -> p (t j)"),
                )

        w_codes = keep.tile([P, row_blocks, passes, P], U32, align_bytes=256)
        w_scales = keep.tile([P, row_blocks, passes, P], U8, align_bytes=256)
        w_grouped = {}

        bank_uses = []

        def next_bank(shape):
            bank_uses.append(shape)
            return bank(shape, len(bank_uses) - 1)

        unread = next_bank([P, T_BLOCK])

        def warm_up(products):
            for i in range(products):
                nc.tensor.matmul(unread[:], zeros[:, 0:P], zeros[:], start=True, stop=True)

        def transpose_w(group):
            w_grouped[group] = keep.tile(
                [P, len(group), passes, P, PACK], BF16, align_bytes=256, name="w_grouped_%d" % group[0]
            )
            for place, b in enumerate(group):
                words = (
                    w_raw[:, b, :]
                    .bitcast(F32)
                    .rearrange("r (c u p) -> r c u p", c=passes, u=HALVES)
                )
                flipped = next_bank([P, passes, HALVES, P])
                for c in range(passes):
                    for u in range(HALVES):
                        nc.tensor.transpose(flipped[:, c, u, :], words[:, c, u, :], identity[:])
                nc.scalar.copy(
                    out=w_grouped[group][:, place].bitcast(F32),
                    in_=flipped[:].rearrange("p c u r -> p c r u"),
                )

        def quantise_w(group):
            lo = w_order.index(group[0])
            hi = lo + len(group)
            nc.vector.quantize_mx(
                out=w_codes[:, lo:hi].rearrange("p b c r -> p (b c r)").bitcast(FP8X4),
                scales=w_scales[:, lo:hi].rearrange("p b c r -> p (b c r)"),
                in_=w_grouped[group][:].rearrange("p b c r j -> p (b c r j)"),
            )

        sums = {}
        pooled = {}
        pooled_out = [out_1[0]] + [out_2[0, r : r + P, :] for r in range(0, Wv.shape[0], P)]

        def multiply_pass(n, blocks, c):
            for b in blocks:
                if c == 0:
                    sums[n, b] = next_bank([P, T_BLOCK])
                nc.tensor.matmul_mx(
                    out=sums[n, b][:],
                    lhsT=w_codes[:, w_order.index(b), c, :].bitcast(FP8X4),
                    lhsT_scale=w_scales[:, w_order.index(b), c, :],
                    rhs=x_codes[:, n, c, :].bitcast(FP8X4),
                    rhs_scale=x_scales[:, n, c, :],
                    start=(c == 0),
                    stop=(c == passes - 1),
                )

        def multiply(n, blocks):
            for b in blocks:
                for c in range(passes):
                    multiply_pass(n, [b], c)

        def multiply_pass_by_pass(n, blocks):
            for c in range(passes):
                multiply_pass(n, blocks, c)

        def empty(n, blocks):
            for b in blocks:
                if b == 0:
                    q_part = keep.tile([P, T_BLOCK], F32, name="q_part_%d" % n)
                    nc.scalar.copy(out=q_part[:], in_=sums[n, 0][:])
                    nc.sync.dma_start(
                        out=out_0[0, :, n * T_BLOCK : (n + 1) * T_BLOCK], in_=q_part[:]
                    )
                    continue
                nc.vector.tensor_reduce(
                    out=pooled[n][:, b - 1, :],
                    in_=sums[n, b][:].rearrange("p (w i) -> p w i", i=WINDOW),
                    axis=mybir.AxisListType.X,
                    op=mybir.AluOpType.max,
                )
                nc.sync.dma_start(
                    out=pooled_out[b - 1][:, n * pooled_cols : (n + 1) * pooled_cols],
                    in_=pooled[n][:, b - 1, :],
                )

        for n in range(rounds):
            pooled[n] = keep.tile([P, row_blocks - 1, pooled_cols], F32, name="pooled_%d" % n)
        regroup_x(0, [0])
        quantise_x(0, [0])
        warm_up(WARM_UP[0])
        transpose_w(W_GROUPS[0])
        warm_up(WARM_UP[1])
        regroup_x(0, [1])
        quantise_w(W_GROUPS[0])
        quantise_x(0, [1])
        transpose_w(W_GROUPS[1])
        regroup_x(1, [0])
        quantise_w(W_GROUPS[1])
        multiply_pass_by_pass(0, [1, 2])
        multiply(0, [3])
        regroup_x(1, [1])
        multiply_pass(0, [4], 0)
        transpose_w(W_GROUPS[2])
        multiply_pass(0, [4], 1)
        empty(0, [1, 2, 3])
        quantise_x(1, range(passes))
        empty(0, [4])
        quantise_w(W_GROUPS[2])
        multiply_pass_by_pass(1, [1, 2])
        multiply(1, [3])
        multiply(0, [5])
        multiply(1, [4])
        multiply(0, [0])
        multiply(1, [5, 0])
        regroup_x(2, range(passes))
        empty(1, [1, 2, 3])
        empty(0, [5])
        quantise_x(2, range(passes))
        regroup_x(3, range(passes))
        multiply_pass_by_pass(2, [1, 2])
        empty(0, [0])
        empty(1, [4])
        multiply(2, [0, 3, 4])
        empty(1, [0, 5])
        multiply(2, [5])
        empty(2, [1, 2])
        quantise_x(3, range(passes))
        multiply(3, [1, 2, 0, 3])
        empty(2, [0])
        multiply(3, [4])
        empty(2, [3])
        multiply(3, [5])
        empty(2, [4, 5])
        empty(3, [1, 2, 0, 3, 4, 5])
